import numpy as np
import ml_dtypes


def mxq(x, axis, fmt="e4m3"):
    dtype, down = {"e4m3": (ml_dtypes.float8_e4m3fn, 7), "e5m2": (ml_dtypes.float8_e5m2, 14)}[fmt]
    v = np.moveaxis(np.asarray(x, np.float32).astype(ml_dtypes.bfloat16).astype(np.float64), axis, -1)
    blocks = v.reshape(v.shape[:-1] + (-1, 32))
    amax = np.abs(blocks).max(-1, keepdims=True)
    byte = np.maximum(np.where(amax > 0, np.frexp(amax)[1] - 1 + 127, 0) - down, 1)
    scale = np.exp2(byte - 127.0)
    codes = (blocks / scale).astype(np.float32).astype(dtype).astype(np.float64)
    return np.moveaxis((codes * scale).reshape(v.shape), -1, axis)


WIDE = False


def mx_kscale(k):
    if not WIDE:
        return np.ones(k)
    levels = np.array([10, -10, 5, -5, 0])
    if k % 512:
        return np.exp2(np.random.permutation(np.resize(levels, k // 32))).repeat(32)
    a = np.empty((k // 512, 16))
    for p in range(k // 512):
        a[p, :8] = np.random.permutation(np.resize(levels, 8))
        for g in range(8):
            far = levels[np.abs(levels - a[p, g]) >= 10]
            a[p, g + 8] = far[np.random.randint(len(far))]
    return np.exp2(a.ravel()).repeat(32)


BF16 = ml_dtypes.bfloat16


def bf(x):
    return np.asarray(x, np.float32).astype(BF16)


def f64(x):
    return np.asarray(x).astype(np.float64)


B, T, C, H, KV, HD, W = 1, 8192, 512, 2, 2, 64, 1024
THETA = 10000.0
HALF = HD // 2


def rope_cos_sin():
    inv = 1.0 / THETA ** (np.arange(HALF) / HALF)
    f = np.arange(T)[:, None] * inv[None, :]
    return np.cos(f), np.sin(f)


def apply_rope(y, cos, sin):
    yr, yi = y[..., 0::2], y[..., 1::2]
    out_r = yr * cos - yi * sin
    out_i = yr * sin + yi * cos
    return np.stack([out_r, out_i], axis=-1).reshape(y.shape)


def draw0():
    s = mx_kscale(C)
    return {"x": bf(np.random.standard_normal((B, T, C)) * s),
            "wq": bf(np.random.standard_normal((C, H * HD)) * 0.8 / np.sqrt(C) / s[:, None]),
            "wk": bf(np.random.standard_normal((C, KV * HD)) * 0.8 / np.sqrt(C) / s[:, None]),
            "wv": bf(np.random.standard_normal((C, KV * HD)) * 2.0 / np.sqrt(C) / s[:, None])}


def core(x, wq, wk, wv):
    xq = mxq(f64(x), 2, "e4m3")
    q = (xq @ mxq(f64(wq), 0, "e4m3")).reshape(B, T, H, HD).transpose(0, 2, 1, 3)
    k = (xq @ mxq(f64(wk), 0, "e4m3")).reshape(B, T, KV, HD).transpose(0, 2, 1, 3)
    v = (xq @ mxq(f64(wv), 0, "e4m3")).reshape(B, T, KV, HD).transpose(0, 2, 1, 3)
    cos, sin = rope_cos_sin()
    return apply_rope(q, cos, sin), apply_rope(k, cos, sin), v


def e4m3fn_bytes(y):
    return np.clip(np.asarray(y, np.float64), -448.0, 448.0).astype(np.float32).astype(ml_dtypes.float8_e4m3fn).view(np.uint8)


def e4m3fn_values(b):
    return np.asarray(b, np.uint8).view(ml_dtypes.float8_e4m3fn).astype(np.float64)


def setup_inputs():
    d = draw0()
    x0 = np.asarray(d['x']).astype(np.float64)
    s = (np.max(np.abs(x0), axis=(0, 1), keepdims=True) / 448.0).astype(np.float32)
    out = {}
    for k, v in d.items():
        if k == 'x':
            out['x_bytes'] = e4m3fn_bytes(x0 / s.astype(np.float64))
            out['x_scale'] = s
        else:
            out[k] = v
    return out


def reference(x_bytes, x_scale, wq, wk, wv):
    return core(e4m3fn_values(x_bytes) * x_scale.astype(np.float64), wq, wk, wv)

@@ -1,0 +1,283 @@
+from contextlib import ExitStack
+
+import concourse.mybir as mybir
+from concourse.masks import make_identity
+
+F32 = mybir.dt.float32
+BF16 = mybir.dt.bfloat16
+I32 = mybir.dt.int32
+U32 = mybir.dt.uint32
+U8 = mybir.dt.uint8
+FP8 = mybir.dt.float8_e4m3fn
+FP8X4 = mybir.dt.float8_e4m3fn_x4
+ALU = mybir.AluOpType
+ACT = mybir.ActivationFunctionType
+
+P = 128
+T = 8192
+K = 512
+NT = 64
+NPAIR = NT // 2
+HALF = 32
+TWO_PI = 6.283185307179586
+HALF_PI = 1.5707963267948966
+
+FLOPS = 2 * T * K * 384
+
+X_CHUNKS = [2, 2, 4, 8, 8, 8, 8, 8, 8, 8]
+TABLE_CHUNKS = [(0, 1, 1), (1, 3, 3), (4, 4, 6), (8, 4, 12), (12, 4, 20)]
+TURN_STEPS = {5: (4,), 10: (5,)}
+QUARTER_PI = 0.7853981633974483
+ROOT2 = 1.4142135623730951
+M_WRAP = 16
+
+
+def split_turns(m):
+    c = 10000.0 ** (-m / 32.0) / TWO_PI
+    q = 1.0
+    for s in range(64):
+        if c * q < 65536.0:
+            q = q * 2.0
+    hi = round(c * q) / q
+    return hi, c - hi
+
+
+def tile_slidingwindowattention_pa_t_kernel(tc, x_bytes, x_scale, wq, wk, wv, out_0, out_1, out_2):
+    nc = tc.nc
+    with ExitStack() as ctx:
+        const = ctx.enter_context(tc.tile_pool(name="const", bufs=1))
+        xin = ctx.enter_context(tc.tile_pool(name="xin", bufs=1))
+        work = ctx.enter_context(tc.tile_pool(name="work", bufs=3))
+        psum = ctx.enter_context(tc.psum_pool(name="psum", bufs=2))
+
+        x_flat = x_bytes.rearrange("o (p i) k -> p (o i k)", i=NT)
+        x_tiles = []
+        first = 0
+        w_raw = const.tile([P, 3, 4, P], BF16, name="w_raw")
+        for c, n in enumerate(X_CHUNKS):
+            xb = xin.tile([P, n * K], U8, name="xbytes%d" % c)
+            nc.sync.dma_start(out=xb[:], in_=x_flat[:, first * K : (first + n) * K])
+            for j in range(n):
+                x_tiles.append((xb, j))
+            first += n
+            if c == 0:
+                for w, src in enumerate((wq, wk, wv)):
+                    nc.sync.dma_start(out=w_raw[:, w], in_=src.rearrange("(p j) c -> p j c", j=4))
+        sc4 = const.tile([P, 4], F32, name="sc4")
+        nc.scalar.dma_start(out=sc4[:], in_=x_scale.rearrange("a b (p t) -> p (a b t)", t=4))
+
+        ones = const.tile([P, 1], F32, name="ones")
+        nc.vector.memset(ones[:], 1.0)
+        warm = const.tile([P, 1], F32, name="warm")
+        nc.scalar.activation(out=warm[:], in_=ones[:], func=ACT.Sin)
+
+        ident = const.tile([P, P], F32, name="ident")
+        make_identity(nc, ident[:])
+        p64 = const.tile([P, 1], F32, name="p64")
+        nc.gpsimd.iota(p64[:], pattern=[[0, 1]], base=0, channel_multiplier=NT, allow_small_or_imprecise_dtypes=True)
+        chi = const.tile([P, HALF], F32, name="chi")
+        clo = const.tile([P, HALF], F32, name="clo")
+        for m in range(HALF):
+            hi, lo = split_turns(m)
+            if m < 16:
+                nc.gpsimd.memset(chi[:, m : m + 1], hi)
+            else:
+                nc.vector.memset(chi[:, m : m + 1], hi)
+            if m < 12:
+                nc.scalar.activation(out=clo[:, m : m + 1], in_=ones[:], func=ACT.Copy, scale=lo)
+            else:
+                nc.vector.tensor_scalar(out=clo[:, m : m + 1], in0=ones[:], scalar1=lo, scalar2=None, op0=ALU.mult)
+
+        t_s = const.tile([P, NT, HALF], F32, name="t_s")
+        c_pow = const.tile([P, 6, HALF], F32, name="c_pow")
+
+        def prepare_angles():
+            u_p = const.tile([P, HALF], F32, name="u_p")
+            nc.vector.tensor_scalar(out=u_p[:], in0=chi[:], scalar1=p64[:, 0:1], scalar2=None, op0=ALU.mult)
+            n_p = const.tile([P, HALF], I32, name="n_p")
+            nc.vector.tensor_copy(out=n_p[:], in_=u_p[:])
+            f_p = const.tile([P, HALF], F32, name="f_p")
+            nc.vector.tensor_tensor(out=f_p[:], in0=u_p[:], in1=n_p[:], op=ALU.subtract)
+            f_p2 = const.tile([P, HALF], F32, name="f_p2")
+            nc.vector.scalar_tensor_tensor(out=f_p2[:], in0=clo[:], scalar=p64[:, 0:1], in1=f_p[:], op0=ALU.mult, op1=ALU.add)
+            f_p3 = const.tile([P, HALF], F32, name="f_p3")
+            nc.vector.tensor_scalar(out=f_p3[:], in0=f_p2[:], scalar1=-0.125, scalar2=None, op0=ALU.add)
+            n_p3 = const.tile([P, HALF], I32, name="n_p3")
+            nc.vector.tensor_copy(out=n_p3[:], in_=f_p3[:])
+            nc.vector.tensor_tensor(out=t_s[:, 0, :], in0=f_p3[:], in1=n_p3[:], op=ALU.subtract)
+            nc.vector.tensor_tensor(out=c_pow[:, 0, :], in0=chi[:], in1=clo[:], op=ALU.add)
+
+        def make_turns(k):
+            n = 2 ** k
+            if k > 0:
+                nc.vector.tensor_scalar(out=c_pow[:, k, :], in0=c_pow[:, 0, :], scalar1=float(n), scalar2=None, op0=ALU.mult)
+            nc.vector.tensor_tensor(out=t_s[:, n : 2 * n, :], in0=t_s[:, 0:n, :], in1=c_pow[:, k, :].unsqueeze(1).to_broadcast([P, n, HALF]), op=ALU.add)
+
+        table = const.tile([P, NT // 4, 3, 4, HALF], F32, name="table")
+
+        wrapped_turns = {}
+
+        def fill_table(turns, g0, ng, m0, m1, wrapped):
+            shape = [P, 4 * ng, m1 - m0]
+            by_group = "p (g i) m -> p g i m"
+            t_b = work.tile(shape, F32, name="t_b", tag="t_b", bufs=2)
+            nc.scalar.activation(out=t_b[:], in_=turns, func=ACT.Abs, bias=QUARTER_PI, scale=TWO_PI)
+            nc.scalar.activation(out=table[:, g0 : g0 + ng, 0, :, m0:m1], in_=t_b[:].rearrange(by_group, i=4), func=ACT.Sin, bias=HALF_PI, scale=-1.0)
+            t_a = work.tile(shape, F32, name="t_a", tag="t_a", bufs=2)
+            nc.scalar.activation(out=t_a[:], in_=turns, func=ACT.Abs)
+            t_nc = work.tile(shape, F32, name="t_nc", tag="t_nc", bufs=2)
+            nc.scalar.activation(out=t_nc[:], in_=t_a[:], func=ACT.Sin, bias=-HALF_PI, scale=TWO_PI)
+            nc.scalar.activation(out=table[:, g0 : g0 + ng, 1, :, m0:m1], in_=t_nc[:].rearrange(by_group, i=4), func=ACT.Copy, scale=ROOT2)
+            t_sn = work.tile(shape, F32, name="t_sn", tag="t_sn", bufs=2)
+            if wrapped:
+                nc.scalar.activation(out=t_sn[:], in_=turns, func=ACT.Sin, scale=TWO_PI)
+            else:
+                t_c = work.tile(shape, F32, name="t_c", tag="t_c", bufs=2)
+                nc.scalar.activation(out=t_c[:], in_=turns, func=ACT.Abs, bias=-HALF_PI, scale=TWO_PI)
+                nc.scalar.activation(out=t_sn[:], in_=t_c[:], func=ACT.Sin, bias=HALF_PI, scale=-1.0)
+            nc.scalar.activation(out=table[:, g0 : g0 + ng, 2, :, m0:m1], in_=t_sn[:].rearrange(by_group, i=4), func=ACT.Copy, scale=ROOT2)
+
+        def wrap_turns(g0, ng):
+            n = 4 * ng
+            i0 = 4 * g0
+            shape = [P, n, M_WRAP]
+            t_n = work.tile(shape, I32, name="t_n", tag="t_n", bufs=2)
+            nc.vector.tensor_copy(out=t_n[:], in_=t_s[:, i0 : i0 + n, 0:M_WRAP])
+            t_d = work.tile(shape, F32, name="t_d", tag="t_d", bufs=2)
+            nc.vector.tensor_tensor(out=t_d[:], in0=t_s[:, i0 : i0 + n, 0:M_WRAP], in1=t_n[:], op=ALU.subtract)
+            wrapped_turns[g0] = t_d
+
+        def make_table(g0, ng):
+            n = 4 * ng
+            i0 = 4 * g0
+            fill_table(wrapped_turns[g0][:], g0, ng, 0, M_WRAP, True)
+            fill_table(t_s[:, i0 : i0 + n, M_WRAP:HALF], g0, ng, M_WRAP, HALF, False)
+
+        prepare_angles()
+        for k in range(4):
+            make_turns(k)
+        wrap_turns(0, 1)
+        wrap_turns(1, 3)
+
+        w_g = const.tile([P, 512 * 4], BF16, name="w_g", align_bytes=64)
+        w_g4 = w_g[:].rearrange("p (c j) -> p c j", j=4)
+        w_codes = const.tile([P, 512], U32, name="w_codes", align_bytes=64)
+        w_scales = const.tile([P, 512], U8, name="w_scales", align_bytes=64)
+
+        def prepare_weights():
+            for e in range(2):
+                nc.vector.tensor_copy(
+                    out=w_g4[:, e * P : (e + 1) * P, :].rearrange("p (w c) j -> p w c j", w=2),
+                    in_=w_raw[:, 0:2].rearrange("p w j (c e) -> p w c j e", e=2)[:, :, :, :, e],
+                )
+            nc.vector.tensor_copy(out=w_g4[:, 384:512, :], in_=w_raw[:, 2].rearrange("p j c -> p c j"))
+            nc.vector.tensor_copy(out=w_g[:, 1024:1536], in_=w_g[:, 0:512])
+            nc.vector.quantize_mx(out=w_codes[:].bitcast(FP8X4), scales=w_scales[:], in_=w_g[:])
+
+        prepare_weights()
+
+        out_views = [o.rearrange("o h (p i) d -> p (o h) i d", i=NT) for o in (out_0, out_1, out_2)]
+
+        state = {}
+
+        def cast(q):
+            xb, j = x_tiles[2 * q]
+            x_bf = work.tile([P, 2 * K], BF16, name="x_bf", tag="x_bf", bufs=4)
+            nc.scalar.copy(out=x_bf[:], in_=xb[:, j * K : (j + 2) * K].bitcast(FP8))
+            state[("x_bf", q)] = x_bf
+
+        def transposes(q):
+            words = state[("x_bf", q)][:].bitcast(F32)
+            x_t = psum.tile([P, 512], F32, name="x_t", tag="x_t", bufs=2)
+            for u in range(2):
+                for j in range(2):
+                    nc.tensor.transpose(x_t[:, (u * 2 + j) * P : (u * 2 + j + 1) * P], words[:, j * 256 + u : (j + 1) * 256 : 2], ident[:])
+            state[("x_t", q)] = x_t
+
+        def scale_mult(q):
+            x_t = state[("x_t", q)]
+            grouped = work.tile([P, 4 * 256], BF16, name="grouped", tag="grouped", bufs=3, align_bytes=64)
+            nc.vector.tensor_tensor(
+                out=grouped[:].rearrange("p (r u e) -> p r u e", u=2, e=2),
+                in0=x_t[:].bitcast(BF16).rearrange("p (u r e) -> p r u e", u=2, e=2),
+                in1=sc4[:].rearrange("p (u e) -> p u e", u=2).unsqueeze(1).to_broadcast([P, 256, 2, 2]),
+                op=ALU.mult,
+            )
+            state[("grouped", q)] = grouped
+
+        def quantize(q):
+            grouped = state[("grouped", q)]
+            codes = work.tile([P, 256], U32, name="codes", tag="codes", bufs=3, align_bytes=64)
+            scales = work.tile([P, 256], U8, name="scales", tag="scales", bufs=3, align_bytes=64)
+            nc.vector.quantize_mx(out=codes[:].bitcast(FP8X4), scales=scales[:], in_=grouped[:])
+            state[("codes", q)] = (codes, scales)
+
+        def matmuls(q):
+            codes, scales = state[("codes", q)]
+            for j in range(2):
+                cols = slice(j * P, (j + 1) * P)
+                y = psum.tile([P, 512], F32, name="y", tag="y", bufs=6)
+                for o0, o1, r0, r1, start, stop in ((0, 128, 0, 128, True, False), (0, 128, 128, 256, False, True), (128, 384, 128, 384, True, True), (384, 512, 384, 512, True, True)):
+                    nc.tensor.matmul_mx(
+                        out=y[:, o0:o1], lhsT=codes[:, cols].bitcast(FP8X4), lhsT_scale=scales[:, cols],
+                        rhs=w_codes[:, r0:r1].bitcast(FP8X4), rhs_scale=w_scales[:, r0:r1], start=start, stop=stop,
+                    )
+                state[("y", 2 * q + j)] = y
+
+        def rope(q):
+            g = q // 2
+            if q % 2 == 0:
+                state["o_qk"] = work.tile([P, 4, 4, 64], F32, name="o_qk", tag="o_qk", bufs=3)
+                state["o_v"] = work.tile([P, 2, 4, 64], F32, name="o_v", tag="o_v", bufs=3)
+            o_qk, o_v = state["o_qk"], state["o_v"]
+            prod = work.tile([P, 3, 4, 2, HALF], F32, name="prod", tag="prod", bufs=3)
+            for j in range(2):
+                il = (q % 2) * 2 + j
+                y = state[("y", 2 * q + j)]
+                nc.vector.tensor_tensor(
+                    out=prod[:, :, :, j, :], in0=y[:, 0:384].rearrange("p (b h m) -> p b h m", b=3, h=4),
+                    in1=table[:, g, :, il, :].unsqueeze(2).to_broadcast([P, 3, 4, HALF]), op=ALU.mult,
+                )
+                nc.scalar.copy(out=o_v[:, :, il, :], in_=y[:, 384:512].rearrange("p (h d) -> p h d", h=2))
+            state[("prod", q)] = prod
+
+        def add(q):
+            g = q // 2
+            o_qk, o_v = state["o_qk"], state["o_v"]
+            prod = state[("prod", q)]
+            l0 = (q % 2) * 2
+            adder = nc.vector if q == NPAIR - 1 else nc.gpsimd
+            adder.tensor_tensor(
+                out=o_qk[:, :, l0 : l0 + 2, :].rearrange("p h i (m e) -> p h (i m) e", e=2),
+                in0=prod[:, 0].rearrange("p h i m -> p h (i m)").unsqueeze(3).to_broadcast([P, 4, 64, 2]),
+                in1=prod[:, 1:3].rearrange("p e h i m -> p h (i m) e"),
+                op=ALU.add,
+            )
+            if q % 2 == 1:
+                i0 = 4 * g
+                nc.sync.dma_start(out=out_views[2][:, :, i0 : i0 + 4, :], in_=o_v[:])
+                nc.sync.dma_start(out=out_views[0][:, :, i0 : i0 + 4, :], in_=o_qk[:, 0:2])
+                nc.sync.dma_start(out=out_views[1][:, :, i0 : i0 + 4, :], in_=o_qk[:, 2:4])
+
+        for step in range(NPAIR + 4):
+            if step < NPAIR:
+                cast(step)
+            if 0 <= step - 1 < NPAIR:
+                transposes(step - 1)
+            if 0 <= step - 3 < NPAIR:
+                matmuls(step - 3)
+            if 0 <= step - 2 < NPAIR:
+                scale_mult(step - 2)
+            for k in TURN_STEPS.get(step, ()):
+                make_turns(k)
+            for g0, ng, when in TABLE_CHUNKS:
+                if when == step:
+                    if g0 >= 4:
+                        wrap_turns(g0, ng)
+                    make_table(g0, ng)
+            if 0 <= step - 4 < NPAIR:
+                rope(step - 4)
+            if 0 <= step - 2 < NPAIR:
+                quantize(step - 2)
+            if 0 <= step - 4 < NPAIR:
+                add(step - 4)

@@ -26,7 +26,6 @@ FLOPS = 2 * T * K * 384
 
 X_CHUNKS = [2, 2, 4, 8, 8, 8, 8, 8, 8, 8]
 TABLE_CHUNKS = [(0, 1, 1), (1, 3, 3), (4, 4, 6), (8, 4, 12), (12, 4, 20)]
-TURN_STEPS = {5: (4,), 10: (5,)}
 QUARTER_PI = 0.7853981633974483
 ROOT2 = 1.4142135623730951
 M_WRAP = 16
@@ -103,78 +102,60 @@ def tile_slidingwindowattention_pa_t_kernel(tc, x_bytes, x_scale, wq, wk, wv, ou
             f_p3 = const.tile([P, HALF], F32, name="f_p3")
             nc.vector.tensor_scalar(out=f_p3[:], in0=f_p2[:], scalar1=-0.125, scalar2=None, op0=ALU.add)
             n_p3 = const.tile([P, HALF], I32, name="n_p3")
-            nc.vector.tensor_copy(out=n_p3[:], in_=f_p3[:])
+            nc.vector.tensor_copy(out=n_p3[:], in_=f_p2[:])
             nc.vector.tensor_tensor(out=t_s[:, 0, :], in0=f_p3[:], in1=n_p3[:], op=ALU.subtract)
             nc.vector.tensor_tensor(out=c_pow[:, 0, :], in0=chi[:], in1=clo[:], op=ALU.add)
 
-        def make_turns(k):
+        def make_turns(k, engine):
             n = 2 ** k
             if k > 0:
                 nc.vector.tensor_scalar(out=c_pow[:, k, :], in0=c_pow[:, 0, :], scalar1=float(n), scalar2=None, op0=ALU.mult)
-            nc.vector.tensor_tensor(out=t_s[:, n : 2 * n, :], in0=t_s[:, 0:n, :], in1=c_pow[:, k, :].unsqueeze(1).to_broadcast([P, n, HALF]), op=ALU.add)
+            engine.tensor_tensor(out=t_s[:, n : 2 * n, :], in0=t_s[:, 0:n, :], in1=c_pow[:, k, :].unsqueeze(1).to_broadcast([P, n, HALF]), op=ALU.add)
 
         table = const.tile([P, NT // 4, 3, 4, HALF], F32, name="table")
-
-        wrapped_turns = {}
-
-        def fill_table(turns, g0, ng, m0, m1, wrapped):
-            shape = [P, 4 * ng, m1 - m0]
-            by_group = "p (g i) m -> p g i m"
-            t_b = work.tile(shape, F32, name="t_b", tag="t_b", bufs=2)
-            nc.scalar.activation(out=t_b[:], in_=turns, func=ACT.Abs, bias=QUARTER_PI, scale=TWO_PI)
-            nc.scalar.activation(out=table[:, g0 : g0 + ng, 0, :, m0:m1], in_=t_b[:].rearrange(by_group, i=4), func=ACT.Sin, bias=HALF_PI, scale=-1.0)
-            t_a = work.tile(shape, F32, name="t_a", tag="t_a", bufs=2)
-            nc.scalar.activation(out=t_a[:], in_=turns, func=ACT.Abs)
-            t_nc = work.tile(shape, F32, name="t_nc", tag="t_nc", bufs=2)
-            nc.scalar.activation(out=t_nc[:], in_=t_a[:], func=ACT.Sin, bias=-HALF_PI, scale=TWO_PI)
-            nc.scalar.activation(out=table[:, g0 : g0 + ng, 1, :, m0:m1], in_=t_nc[:].rearrange(by_group, i=4), func=ACT.Copy, scale=ROOT2)
-            t_sn = work.tile(shape, F32, name="t_sn", tag="t_sn", bufs=2)
-            if wrapped:
-                nc.scalar.activation(out=t_sn[:], in_=turns, func=ACT.Sin, scale=TWO_PI)
-            else:
-                t_c = work.tile(shape, F32, name="t_c", tag="t_c", bufs=2)
-                nc.scalar.activation(out=t_c[:], in_=turns, func=ACT.Abs, bias=-HALF_PI, scale=TWO_PI)
-                nc.scalar.activation(out=t_sn[:], in_=t_c[:], func=ACT.Sin, bias=HALF_PI, scale=-1.0)
-            nc.scalar.activation(out=table[:, g0 : g0 + ng, 2, :, m0:m1], in_=t_sn[:].rearrange(by_group, i=4), func=ACT.Copy, scale=ROOT2)
 
         def wrap_turns(g0, ng):
             n = 4 * ng
             i0 = 4 * g0
-            shape = [P, n, M_WRAP]
-            t_n = work.tile(shape, I32, name="t_n", tag="t_n", bufs=2)
+            t_n = work.tile([P, n, M_WRAP], I32, name="t_n", tag="t_n", bufs=2)
             nc.vector.tensor_copy(out=t_n[:], in_=t_s[:, i0 : i0 + n, 0:M_WRAP])
-            t_d = work.tile(shape, F32, name="t_d", tag="t_d", bufs=2)
-            nc.vector.tensor_tensor(out=t_d[:], in0=t_s[:, i0 : i0 + n, 0:M_WRAP], in1=t_n[:], op=ALU.subtract)
-            wrapped_turns[g0] = t_d
+            nc.vector.tensor_tensor(out=t_s[:, i0 : i0 + n, 0:M_WRAP], in0=t_s[:, i0 : i0 + n, 0:M_WRAP], in1=t_n[:], op=ALU.subtract)
 
         def make_table(g0, ng):
             n = 4 * ng
             i0 = 4 * g0
-            fill_table(wrapped_turns[g0][:], g0, ng, 0, M_WRAP, True)
-            fill_table(t_s[:, i0 : i0 + n, M_WRAP:HALF], g0, ng, M_WRAP, HALF, False)
+            folded = work.tile([P, ng, 3, 4, HALF], F32, name="folded", tag="folded", bufs=2)
+            for b, beta in enumerate((QUARTER_PI, 0.0, HALF_PI)):
+                nc.scalar.activation(out=folded[:, :, b], in_=t_s[:, i0 : i0 + n, :].rearrange("p (g i) m -> p g i m", i=4), func=ACT.Abs, bias=beta, scale=TWO_PI)
+            nc.scalar.activation(out=table[:, g0 : g0 + ng], in_=folded[:], func=ACT.Sin, bias=-HALF_PI, scale=1.0)
+            nc.scalar.activation(out=table[:, g0 : g0 + ng, 1:3], in_=table[:, g0 : g0 + ng, 1:3], func=ACT.Copy, scale=ROOT2)
 
         prepare_angles()
         for k in range(4):
-            make_turns(k)
+            make_turns(k, nc.vector)
         wrap_turns(0, 1)
         wrap_turns(1, 3)
 
-        w_g = const.tile([P, 512 * 4], BF16, name="w_g", align_bytes=64)
+        w_g = const.tile([P, 384 * 4], BF16, name="w_g", align_bytes=64)
         w_g4 = w_g[:].rearrange("p (c j) -> p c j", j=4)
-        w_codes = const.tile([P, 512], U32, name="w_codes", align_bytes=64)
-        w_scales = const.tile([P, 512], U8, name="w_scales", align_bytes=64)
+        w_codes = const.tile([P, 384], U32, name="w_codes", align_bytes=64)
+        w_scales = const.tile([P, 384], U8, name="w_scales", align_bytes=64)
 
         def prepare_weights():
             for e in range(2):
-                nc.vector.tensor_copy(
-                    out=w_g4[:, e * P : (e + 1) * P, :].rearrange("p (w c) j -> p w c j", w=2),
-                    in_=w_raw[:, 0:2].rearrange("p w j (c e) -> p w c j e", e=2)[:, :, :, :, e],
+                block = 1 - e
+                nc.gpsimd.tensor_scalar(
+                    out=w_g4[:, block * P : (block + 1) * P, :].rearrange("p (w c) j -> p w c j", w=2),
+                    in0=w_raw[:, 0:2].rearrange("p w j (c e) -> p w c j e", e=2)[:, :, :, :, e],
+                    scalar1=1.0, scalar2=0.0, op0=ALU.mult, op1=ALU.add,
                 )
-            nc.vector.tensor_copy(out=w_g4[:, 384:512, :], in_=w_raw[:, 2].rearrange("p j c -> p c j"))
-            nc.vector.tensor_copy(out=w_g[:, 1024:1536], in_=w_g[:, 0:512])
-            nc.vector.quantize_mx(out=w_codes[:].bitcast(FP8X4), scales=w_scales[:], in_=w_g[:])
+            nc.gpsimd.tensor_scalar(out=w_g4[:, 256:384, :], in0=w_raw[:, 2].rearrange("p j c -> p c j"), scalar1=1.0, scalar2=0.0, op0=ALU.mult, op1=ALU.add)
+            nc.vector.quantize_mx(out=w_codes[:, 0:256].bitcast(FP8X4), scales=w_scales[:, 0:256], in_=w_g[:, 0:1024])
+            nc.vector.quantize_mx(out=w_codes[:, 256:384].bitcast(FP8X4), scales=w_scales[:, 256:384], in_=w_g[:, 1024:1536])
 
         prepare_weights()
+        for k in range(4, 6):
+            make_turns(k, nc.gpsimd)
 
         out_views = [o.rearrange("o h (p i) d -> p (o h) i d", i=NT) for o in (out_0, out_1, out_2)]
 
@@ -217,7 +198,7 @@ def tile_slidingwindowattention_pa_t_kernel(tc, x_bytes, x_scale, wq, wk, wv, ou
             for j in range(2):
                 cols = slice(j * P, (j + 1) * P)
                 y = psum.tile([P, 512], F32, name="y", tag="y", bufs=6)
-                for o0, o1, r0, r1, start, stop in ((0, 128, 0, 128, True, False), (0, 128, 128, 256, False, True), (128, 384, 128, 384, True, True), (384, 512, 384, 512, True, True)):
+                for o0, o1, r0, r1, start, stop in ((0, 128, 0, 128, True, False), (0, 128, 128, 256, False, True), (128, 384, 0, 256, True, True), (384, 512, 256, 384, True, True)):
                     nc.tensor.matmul_mx(
                         out=y[:, o0:o1], lhsT=codes[:, cols].bitcast(FP8X4), lhsT_scale=scales[:, cols],
                         rhs=w_codes[:, r0:r1].bitcast(FP8X4), rhs_scale=w_scales[:, r0:r1], start=start, stop=stop,
@@ -249,9 +230,9 @@ def tile_slidingwindowattention_pa_t_kernel(tc, x_bytes, x_scale, wq, wk, wv, ou
             adder = nc.vector if q == NPAIR - 1 else nc.gpsimd
             adder.tensor_tensor(
                 out=o_qk[:, :, l0 : l0 + 2, :].rearrange("p h i (m e) -> p h (i m) e", e=2),
-                in0=prod[:, 0].rearrange("p h i m -> p h (i m)").unsqueeze(3).to_broadcast([P, 4, 64, 2]),
-                in1=prod[:, 1:3].rearrange("p e h i m -> p h (i m) e"),
-                op=ALU.add,
+                in0=prod[:, 1:3].rearrange("p e h i m -> p h (i m) e"),
+                in1=prod[:, 0].rearrange("p h i m -> p h (i m)").unsqueeze(3).to_broadcast([P, 4, 64, 2]),
+                op=ALU.subtract,
             )
             if q % 2 == 1:
                 i0 = 4 * g
@@ -268,8 +249,6 @@ def tile_slidingwindowattention_pa_t_kernel(tc, x_bytes, x_scale, wq, wk, wv, ou
                 matmuls(step - 3)
             if 0 <= step - 2 < NPAIR:
                 scale_mult(step - 2)
-            for k in TURN_STEPS.get(step, ()):
-                make_turns(k)
             for g0, ng, when in TABLE_CHUNKS:
                 if when == step:
                     if g0 >= 4:

@@ -172,7 +172,7 @@ def tile_slidingwindowattention_pa_t_kernel(tc, x_bytes, x_scale, wq, wk, wv, ou
             x_t = psum.tile([P, 512], F32, name="x_t", tag="x_t", bufs=2)
             for u in range(2):
                 for j in range(2):
-                    nc.tensor.transpose(x_t[:, (u * 2 + j) * P : (u * 2 + j + 1) * P], words[:, j * 256 + u : (j + 1) * 256 : 2], ident[:])
+                    nc.tensor.transpose(x_t[:].rearrange("p (r u) -> p u r", u=2)[:, u, j * P : (j + 1) * P], words[:, j * 256 + u : (j + 1) * 256 : 2], ident[:])
             state[("x_t", q)] = x_t
 
         def scale_mult(q):
@@ -180,7 +180,7 @@ def tile_slidingwindowattention_pa_t_kernel(tc, x_bytes, x_scale, wq, wk, wv, ou
             grouped = work.tile([P, 4 * 256], BF16, name="grouped", tag="grouped", bufs=3, align_bytes=64)
             nc.vector.tensor_tensor(
                 out=grouped[:].rearrange("p (r u e) -> p r u e", u=2, e=2),
-                in0=x_t[:].bitcast(BF16).rearrange("p (u r e) -> p r u e", u=2, e=2),
+                in0=x_t[:].bitcast(BF16).rearrange("p (r u e) -> p r u e", u=2, e=2),
                 in1=sc4[:].rearrange("p (u e) -> p u e", u=2).unsqueeze(1).to_broadcast([P, 256, 2, 2]),
                 op=ALU.mult,
             )

from contextlib import ExitStack

import concourse.mybir as mybir
from concourse.masks import make_identity

F32 = mybir.dt.float32
BF16 = mybir.dt.bfloat16
I32 = mybir.dt.int32
U32 = mybir.dt.uint32
U8 = mybir.dt.uint8
FP8 = mybir.dt.float8_e4m3fn
FP8X4 = mybir.dt.float8_e4m3fn_x4
ALU = mybir.AluOpType
ACT = mybir.ActivationFunctionType

P = 128
T = 8192
K = 512
NT = 64
NPAIR = NT // 2
HALF = 32
TWO_PI = 6.283185307179586
HALF_PI = 1.5707963267948966

FLOPS = 2 * T * K * 384

X_CHUNKS = [2, 2, 4, 8, 8, 8, 8, 8, 8, 8]
TABLE_CHUNKS = [(0, 1, 1), (1, 3, 3), (4, 4, 6), (8, 4, 12), (12, 4, 20)]
QUARTER_PI = 0.7853981633974483
ROOT2 = 1.4142135623730951
M_WRAP = 16


def split_turns(m):
    c = 10000.0 ** (-m / 32.0) / TWO_PI
    q = 1.0
    for s in range(64):
        if c * q < 65536.0:
            q = q * 2.0
    hi = round(c * q) / q
    return hi, c - hi


def tile_slidingwindowattention_pa_t_kernel(tc, x_bytes, x_scale, wq, wk, wv, out_0, out_1, out_2):
    nc = tc.nc
    with ExitStack() as ctx:
        const = ctx.enter_context(tc.tile_pool(name="const", bufs=1))
        xin = ctx.enter_context(tc.tile_pool(name="xin", bufs=1))
        work = ctx.enter_context(tc.tile_pool(name="work", bufs=3))
        psum = ctx.enter_context(tc.psum_pool(name="psum", bufs=2))

        x_flat = x_bytes.rearrange("o (p i) k -> p (o i k)", i=NT)
        x_tiles = []
        first = 0
        w_raw = const.tile([P, 3, 4, P], BF16, name="w_raw")
        for c, n in enumerate(X_CHUNKS):
            xb = xin.tile([P, n * K], U8, name="xbytes%d" % c)
            nc.sync.dma_start(out=xb[:], in_=x_flat[:, first * K : (first + n) * K])
            for j in range(n):
                x_tiles.append((xb, j))
            first += n
            if c == 0:
                for w, src in enumerate((wq, wk, wv)):
                    nc.sync.dma_start(out=w_raw[:, w], in_=src.rearrange("(p j) c -> p j c", j=4))
        sc4 = const.tile([P, 4], F32, name="sc4")
        nc.scalar.dma_start(out=sc4[:], in_=x_scale.rearrange("a b (p t) -> p (a b t)", t=4))

        ones = const.tile([P, 1], F32, name="ones")
        nc.vector.memset(ones[:], 1.0)
        warm = const.tile([P, 1], F32, name="warm")
        nc.scalar.activation(out=warm[:], in_=ones[:], func=ACT.Sin)

        ident = const.tile([P, P], F32, name="ident")
        make_identity(nc, ident[:])
        p64 = const.tile([P, 1], F32, name="p64")
        nc.gpsimd.iota(p64[:], pattern=[[0, 1]], base=0, channel_multiplier=NT, allow_small_or_imprecise_dtypes=True)
        chi = const.tile([P, HALF], F32, name="chi")
        clo = const.tile([P, HALF], F32, name="clo")
        for m in range(HALF):
            hi, lo = split_turns(m)
            if m < 16:
                nc.gpsimd.memset(chi[:, m : m + 1], hi)
            else:
                nc.vector.memset(chi[:, m : m + 1], hi)
            if m < 12:
                nc.scalar.activation(out=clo[:, m : m + 1], in_=ones[:], func=ACT.Copy, scale=lo)
            else:
                nc.vector.tensor_scalar(out=clo[:, m : m + 1], in0=ones[:], scalar1=lo, scalar2=None, op0=ALU.mult)

        t_s = const.tile([P, NT, HALF], F32, name="t_s")
        c_pow = const.tile([P, 6, HALF], F32, name="c_pow")

        def prepare_angles():
            u_p = const.tile([P, HALF], F32, name="u_p")
            nc.vector.tensor_scalar(out=u_p[:], in0=chi[:], scalar1=p64[:, 0:1], scalar2=None, op0=ALU.mult)
            n_p = const.tile([P, HALF], I32, name="n_p")
            nc.vector.tensor_copy(out=n_p[:], in_=u_p[:])
            f_p = const.tile([P, HALF], F32, name="f_p")
            nc.vector.tensor_tensor(out=f_p[:], in0=u_p[:], in1=n_p[:], op=ALU.subtract)
            f_p2 = const.tile([P, HALF], F32, name="f_p2")
            nc.vector.scalar_tensor_tensor(out=f_p2[:], in0=clo[:], scalar=p64[:, 0:1], in1=f_p[:], op0=ALU.mult, op1=ALU.add)
            f_p3 = const.tile([P, HALF], F32, name="f_p3")
            nc.vector.tensor_scalar(out=f_p3[:], in0=f_p2[:], scalar1=-0.125, scalar2=None, op0=ALU.add)
            n_p3 = const.tile([P, HALF], I32, name="n_p3")
            nc.vector.tensor_copy(out=n_p3[:], in_=f_p2[:])
            nc.vector.tensor_tensor(out=t_s[:, 0, :], in0=f_p3[:], in1=n_p3[:], op=ALU.subtract)
            nc.vector.tensor_tensor(out=c_pow[:, 0, :], in0=chi[:], in1=clo[:], op=ALU.add)

        def make_turns(k, engine):
            n = 2 ** k
            if k > 0:
                nc.vector.tensor_scalar(out=c_pow[:, k, :], in0=c_pow[:, 0, :], scalar1=float(n), scalar2=None, op0=ALU.mult)
            engine.tensor_tensor(out=t_s[:, n : 2 * n, :], in0=t_s[:, 0:n, :], in1=c_pow[:, k, :].unsqueeze(1).to_broadcast([P, n, HALF]), op=ALU.add)

        table = const.tile([P, NT // 4, 3, 4, HALF], F32, name="table")

        def wrap_turns(g0, ng):
            n = 4 * ng
            i0 = 4 * g0
            t_n = work.tile([P, n, M_WRAP], I32, name="t_n", tag="t_n", bufs=2)
            nc.vector.tensor_copy(out=t_n[:], in_=t_s[:, i0 : i0 + n, 0:M_WRAP])
            nc.vector.tensor_tensor(out=t_s[:, i0 : i0 + n, 0:M_WRAP], in0=t_s[:, i0 : i0 + n, 0:M_WRAP], in1=t_n[:], op=ALU.subtract)

        def make_table(g0, ng):
            n = 4 * ng
            i0 = 4 * g0
            folded = work.tile([P, ng, 3, 4, HALF], F32, name="folded", tag="folded", bufs=2)
            for b, beta in enumerate((QUARTER_PI, 0.0, HALF_PI)):
                nc.scalar.activation(out=folded[:, :, b], in_=t_s[:, i0 : i0 + n, :].rearrange("p (g i) m -> p g i m", i=4), func=ACT.Abs, bias=beta, scale=TWO_PI)
            nc.scalar.activation(out=table[:, g0 : g0 + ng], in_=folded[:], func=ACT.Sin, bias=-HALF_PI, scale=1.0)
            nc.scalar.activation(out=table[:, g0 : g0 + ng, 1:3], in_=table[:, g0 : g0 + ng, 1:3], func=ACT.Copy, scale=ROOT2)

        prepare_angles()
        for k in range(4):
            make_turns(k, nc.vector)
        wrap_turns(0, 1)
        wrap_turns(1, 3)

        w_g = const.tile([P, 384 * 4], BF16, name="w_g", align_bytes=64)
        w_g4 = w_g[:].rearrange("p (c j) -> p c j", j=4)
        w_codes = const.tile([P, 384], U32, name="w_codes", align_bytes=64)
        w_scales = const.tile([P, 384], U8, name="w_scales", align_bytes=64)

        def prepare_weights():
            for e in range(2):
                block = 1 - e
                nc.gpsimd.tensor_scalar(
                    out=w_g4[:, block * P : (block + 1) * P, :].rearrange("p (w c) j -> p w c j", w=2),
                    in0=w_raw[:, 0:2].rearrange("p w j (c e) -> p w c j e", e=2)[:, :, :, :, e],
                    scalar1=1.0, scalar2=0.0, op0=ALU.mult, op1=ALU.add,
                )
            nc.gpsimd.tensor_scalar(out=w_g4[:, 256:384, :], in0=w_raw[:, 2].rearrange("p j c -> p c j"), scalar1=1.0, scalar2=0.0, op0=ALU.mult, op1=ALU.add)
            nc.vector.quantize_mx(out=w_codes[:, 0:256].bitcast(FP8X4), scales=w_scales[:, 0:256], in_=w_g[:, 0:1024])
            nc.vector.quantize_mx(out=w_codes[:, 256:384].bitcast(FP8X4), scales=w_scales[:, 256:384], in_=w_g[:, 1024:1536])

        prepare_weights()
        for k in range(4, 6):
            make_turns(k, nc.gpsimd)

        out_views = [o.rearrange("o h (p i) d -> p (o h) i d", i=NT) for o in (out_0, out_1, out_2)]

        state = {}

        def cast(q):
            xb, j = x_tiles[2 * q]
            x_bf = work.tile([P, 2 * K], BF16, name="x_bf", tag="x_bf", bufs=4)
            nc.scalar.copy(out=x_bf[:], in_=xb[:, j * K : (j + 2) * K].bitcast(FP8))
            state[("x_bf", q)] = x_bf

        def transposes(q):
            words = state[("x_bf", q)][:].bitcast(F32)
            x_t = psum.tile([P, 512], F32, name="x_t", tag="x_t", bufs=2)
            for u in range(2):
                for j in range(2):
                    nc.tensor.transpose(x_t[:].rearrange("p (r u) -> p u r", u=2)[:, u, j * P : (j + 1) * P], words[:, j * 256 + u : (j + 1) * 256 : 2], ident[:])
            state[("x_t", q)] = x_t

        def scale_mult(q):
            x_t = state[("x_t", q)]
            grouped = work.tile([P, 4 * 256], BF16, name="grouped", tag="grouped", bufs=3, align_bytes=64)
            nc.vector.tensor_tensor(
                out=grouped[:].rearrange("p (r u e) -> p r u e", u=2, e=2),
                in0=x_t[:].bitcast(BF16).rearrange("p (r u e) -> p r u e", u=2, e=2),
                in1=sc4[:].rearrange("p (u e) -> p u e", u=2).unsqueeze(1).to_broadcast([P, 256, 2, 2]),
                op=ALU.mult,
            )
            state[("grouped", q)] = grouped

        def quantize(q):
            grouped = state[("grouped", q)]
            codes = work.tile([P, 256], U32, name="codes", tag="codes", bufs=3, align_bytes=64)
            scales = work.tile([P, 256], U8, name="scales", tag="scales", bufs=3, align_bytes=64)
            nc.vector.quantize_mx(out=codes[:].bitcast(FP8X4), scales=scales[:], in_=grouped[:])
            state[("codes", q)] = (codes, scales)

        def matmuls(q):
            codes, scales = state[("codes", q)]
            for j in range(2):
                cols = slice(j * P, (j + 1) * P)
                y = psum.tile([P, 512], F32, name="y", tag="y", bufs=6)
                for o0, o1, r0, r1, start, stop in ((0, 128, 0, 128, True, False), (0, 128, 128, 256, False, True), (128, 384, 0, 256, True, True), (384, 512, 256, 384, True, True)):
                    nc.tensor.matmul_mx(
                        out=y[:, o0:o1], lhsT=codes[:, cols].bitcast(FP8X4), lhsT_scale=scales[:, cols],
                        rhs=w_codes[:, r0:r1].bitcast(FP8X4), rhs_scale=w_scales[:, r0:r1], start=start, stop=stop,
                    )
                state[("y", 2 * q + j)] = y

        def rope(q):
            g = q // 2
            if q % 2 == 0:
                state["o_qk"] = work.tile([P, 4, 4, 64], F32, name="o_qk", tag="o_qk", bufs=3)
                state["o_v"] = work.tile([P, 2, 4, 64], F32, name="o_v", tag="o_v", bufs=3)
            o_qk, o_v = state["o_qk"], state["o_v"]
            prod = work.tile([P, 3, 4, 2, HALF], F32, name="prod", tag="prod", bufs=3)
            for j in range(2):
                il = (q % 2) * 2 + j
                y = state[("y", 2 * q + j)]
                nc.vector.tensor_tensor(
                    out=prod[:, :, :, j, :], in0=y[:, 0:384].rearrange("p (b h m) -> p b h m", b=3, h=4),
                    in1=table[:, g, :, il, :].unsqueeze(2).to_broadcast([P, 3, 4, HALF]), op=ALU.mult,
                )
                nc.scalar.copy(out=o_v[:, :, il, :], in_=y[:, 384:512].rearrange("p (h d) -> p h d", h=2))
            state[("prod", q)] = prod

        def add(q):
            g = q // 2
            o_qk, o_v = state["o_qk"], state["o_v"]
            prod = state[("prod", q)]
            l0 = (q % 2) * 2
            adder = nc.vector if q == NPAIR - 1 else nc.gpsimd
            adder.tensor_tensor(
                out=o_qk[:, :, l0 : l0 + 2, :].rearrange("p h i (m e) -> p h (i m) e", e=2),
                in0=prod[:, 1:3].rearrange("p e h i m -> p h (i m) e"),
                in1=prod[:, 0].rearrange("p h i m -> p h (i m)").unsqueeze(3).to_broadcast([P, 4, 64, 2]),
                op=ALU.subtract,
            )
            if q % 2 == 1:
                i0 = 4 * g
                nc.sync.dma_start(out=out_views[2][:, :, i0 : i0 + 4, :], in_=o_v[:])
                nc.sync.dma_start(out=out_views[0][:, :, i0 : i0 + 4, :], in_=o_qk[:, 0:2])
                nc.sync.dma_start(out=out_views[1][:, :, i0 : i0 + 4, :], in_=o_qk[:, 2:4])

        for step in range(NPAIR + 4):
            if step < NPAIR:
                cast(step)
            if 0 <= step - 1 < NPAIR:
                transposes(step - 1)
            if 0 <= step - 3 < NPAIR:
                matmuls(step - 3)
            if 0 <= step - 2 < NPAIR:
                scale_mult(step - 2)
            for g0, ng, when in TABLE_CHUNKS:
                if when == step:
                    if g0 >= 4:
                        wrap_turns(g0, ng)
                    make_table(g0, ng)
            if 0 <= step - 4 < NPAIR:
                rope(step - 4)
            if 0 <= step - 2 < NPAIR:
                quantize(step - 2)
            if 0 <= step - 4 < NPAIR:
                add(step - 4)
